import numpy as np
import ml_dtypes

BF16 = ml_dtypes.bfloat16


def bf(x):
    return np.asarray(x, np.float32).astype(BF16)


def f32(x):
    return np.asarray(x, np.float32)


def f64(x):
    return np.asarray(x).astype(np.float64)


def striped(idx):
    return np.tile(idx.reshape(-1, 16).T, (8, 1))


C, R, S, N = 1024, 256, 256, 128


def sigmoid(v):
    return 1.0 / (1.0 + np.exp(-v))


def setup_inputs():
    return {"table": f32(0.5 * np.random.standard_normal((C, S))), "pos": f32(0.5 * np.random.standard_normal((C, N))), "w1": bf(1.5 * np.random.standard_normal((C, R)) / np.sqrt(C)), "b1": f32(0.2 * np.random.standard_normal((R, 1))), "w2": bf(2.0 * np.random.standard_normal((R, C)) / np.sqrt(R)), "b2": f32(0.2 * np.random.standard_normal((C, 1))), "offs": striped(np.random.permutation(np.tile(np.arange(S), 2))[:N])}


def reference(table, pos, w1, b1, w2, b2, offs):
    idx = offs[:16].T.reshape(-1)
    x = f64(table)[:, idx] + f64(pos)
    h = np.tanh(f64(w1).T @ x + f64(b1))
    gate = sigmoid(f64(w2).T @ h + f64(b2))
    return np.concatenate([x, gate], axis=0)

@@ -1,0 +1,90 @@
+import concourse.mybir as mybir
+
+F32, BF16, U16 = mybir.dt.float32, mybir.dt.bfloat16, mybir.dt.uint16
+ADD = mybir.AluOpType.add
+TANH = mybir.ActivationFunctionType.Tanh
+SIGMOID = mybir.ActivationFunctionType.Sigmoid
+
+P = 128
+C, R, S, N = 1024, 256, 256, 128
+KB = C // P
+TB = R // P
+HALF = KB // 2
+
+FLOPS = 2 * C * R * N * 2
+
+
+def tile_quantumtransformer_kernel(tc, table, pos, w1, b1, w2, b2, offs, out):
+    nc = tc.nc
+
+    table_v = table.rearrange("(p k) s -> p k s", k=KB)
+    pos_v = pos.rearrange("(p k) j -> p k j", k=KB)
+    w1_v = w1.rearrange("(p k) (m t) -> p k m t", k=KB, t=TB)
+    w2_v = w2.rearrange("(p t) (m k) -> p t m k", t=TB, k=KB)
+    b1_v = b1.rearrange("(p t) one -> p (t one)", t=TB)
+    b2_v = b2.rearrange("(p k) one -> p (k one)", k=KB)
+    x_out_v = out[0:C, :].rearrange("(p k) j -> p k j", k=KB)
+    gate_out_v = out[C : 2 * C, :].rearrange("(p k) j -> p k j", k=KB)
+
+    with (
+        tc.tile_pool(name="held", bufs=1) as held,
+        tc.psum_pool(name="h_psum", bufs=1) as h_psum,
+        tc.psum_pool(name="g_psum", bufs=4) as g_psum,
+    ):
+        offsets = held.tile([P, N // 16], U16, name="offsets")
+        table_sb = [held.tile([P, S], F32, name=f"table{k}") for k in range(KB)]
+        pos_sb = held.tile([P, KB, N], F32, name="pos_sb")
+        w1_sb = held.tile([P, KB, P, TB], BF16, name="w1_sb")
+        w2_sb = held.tile([P, TB, P, KB], BF16, name="w2_sb")
+        b1_sb = held.tile([P, TB], F32, name="b1_sb")
+        b2_sb = held.tile([P, KB], F32, name="b2_sb")
+        x_sb = held.tile([P, KB, N], F32, name="x_sb")
+        x_bf = held.tile([P, KB, N], BF16, name="x_bf")
+        h_bf = held.tile([P, TB, N], BF16, name="h_bf")
+        gate_sb = held.tile([P, KB, N], F32, name="gate_sb")
+
+        nc.sync.dma_start(offsets[:], offs)
+        nc.sync.dma_start(pos_sb[:, 0:HALF, :], pos_v[:, 0:HALF, :])
+        nc.scalar.dma_start(table_sb[0][:], table_v[:, 0, :])
+        nc.gpsimd.dma_start(w1_sb[:], w1_v)
+        nc.sync.dma_start(table_sb[1][:], table_v[:, 1, :])
+        nc.scalar.dma_start(table_sb[2][:], table_v[:, 2, :])
+        nc.sync.dma_start(table_sb[3][:], table_v[:, 3, :])
+        nc.scalar.dma_start(pos_sb[:, HALF:KB, :], pos_v[:, HALF:KB, :])
+        nc.gpsimd.dma_start(b1_sb[:], b1_v)
+        nc.gpsimd.dma_start(b2_sb[:], b2_v)
+        nc.sync.dma_start(table_sb[5][:], table_v[:, 5, :])
+        nc.scalar.dma_start(table_sb[4][:], table_v[:, 4, :])
+        nc.sync.dma_start(table_sb[7][:], table_v[:, 7, :])
+        nc.scalar.dma_start(table_sb[6][:], table_v[:, 6, :])
+        nc.gpsimd.dma_start(w2_sb[:], w2_v)
+
+        h_ps = [h_psum.tile([P, N], F32, name=f"h_ps{t}") for t in range(TB)]
+        for k in range(KB):
+            nc.vector.tensor_tensor(
+                x_sb[:, k, :], table_sb[k][:].indirect(offsets[:]), pos_sb[:, k, :], ADD
+            )
+            nc.scalar.copy(x_bf[:, k, :], x_sb[:, k, :])
+            for t in range(TB):
+                nc.tensor.matmul(
+                    h_ps[t][:], w1_sb[:, k, :, t], x_bf[:, k, :],
+                    start=(k == 0), stop=(k == KB - 1),
+                )
+            if k % HALF == HALF - 1:
+                blocks = slice(k + 1 - HALF, k + 1)
+                nc.sync.dma_start(x_out_v[:, blocks, :], x_sb[:, blocks, :])
+
+        for t in range(TB):
+            nc.scalar.activation(h_bf[:, t, :], h_ps[t][:], TANH, bias=b1_sb[:, t : t + 1])
+
+        for k in range(KB):
+            g_ps = g_psum.tile([P, N], F32, name="g_ps")
+            for t in range(TB):
+                nc.tensor.matmul(
+                    g_ps[:], w2_sb[:, t, :, k], h_bf[:, t, :],
+                    start=(t == 0), stop=(t == TB - 1),
+                )
+            nc.scalar.activation(gate_sb[:, k, :], g_ps[:], SIGMOID, bias=b2_sb[:, k : k + 1])
+            if k % HALF == HALF - 1:
+                blocks = slice(k + 1 - HALF, k + 1)
+                nc.sync.dma_start(gate_out_v[:, blocks, :], gate_sb[:, blocks, :])

@@ -44,20 +44,21 @@ def tile_quantumtransformer_kernel(tc, table, pos, w1, b1, w2, b2, offs, out):
         gate_sb = held.tile([P, KB, N], F32, name="gate_sb")
 
         nc.sync.dma_start(offsets[:], offs)
+        nc.gpsimd.dma_start(b1_sb[:], b1_v)
+        nc.gpsimd.dma_start(b2_sb[:], b2_v)
         nc.sync.dma_start(pos_sb[:, 0:HALF, :], pos_v[:, 0:HALF, :])
         nc.scalar.dma_start(table_sb[0][:], table_v[:, 0, :])
-        nc.gpsimd.dma_start(w1_sb[:], w1_v)
         nc.sync.dma_start(table_sb[1][:], table_v[:, 1, :])
         nc.scalar.dma_start(table_sb[2][:], table_v[:, 2, :])
         nc.sync.dma_start(table_sb[3][:], table_v[:, 3, :])
-        nc.scalar.dma_start(pos_sb[:, HALF:KB, :], pos_v[:, HALF:KB, :])
-        nc.gpsimd.dma_start(b1_sb[:], b1_v)
-        nc.gpsimd.dma_start(b2_sb[:], b2_v)
-        nc.sync.dma_start(table_sb[5][:], table_v[:, 5, :])
+        nc.scalar.dma_start(w1_sb[:], w1_v)
+        nc.sync.dma_start(pos_sb[:, HALF:KB, :], pos_v[:, HALF:KB, :])
         nc.scalar.dma_start(table_sb[4][:], table_v[:, 4, :])
-        nc.sync.dma_start(table_sb[7][:], table_v[:, 7, :])
+        nc.sync.dma_start(table_sb[5][:], table_v[:, 5, :])
         nc.scalar.dma_start(table_sb[6][:], table_v[:, 6, :])
-        nc.gpsimd.dma_start(w2_sb[:], w2_v)
+        nc.sync.dma_start(table_sb[7][:], table_v[:, 7, :])
+        nc.scalar.dma_start(w2_sb[:, 0, :, :], w2_v[:, 0, :, :])
+        nc.sync.dma_start(w2_sb[:, 1, :, :], w2_v[:, 1, :, :])
 
         h_ps = [h_psum.tile([P, N], F32, name=f"h_ps{t}") for t in range(TB)]
         for k in range(KB):
@@ -70,9 +71,8 @@ def tile_quantumtransformer_kernel(tc, table, pos, w1, b1, w2, b2, offs, out):
                     h_ps[t][:], w1_sb[:, k, :, t], x_bf[:, k, :],
                     start=(k == 0), stop=(k == KB - 1),
                 )
-            if k % HALF == HALF - 1:
-                blocks = slice(k + 1 - HALF, k + 1)
-                nc.sync.dma_start(x_out_v[:, blocks, :], x_sb[:, blocks, :])
+
+        nc.sync.dma_start(x_out_v, x_sb[:])
 
         for t in range(TB):
             nc.scalar.activation(h_bf[:, t, :], h_ps[t][:], TANH, bias=b1_sb[:, t : t + 1])

@@ -44,21 +44,18 @@ def tile_quantumtransformer_kernel(tc, table, pos, w1, b1, w2, b2, offs, out):
         gate_sb = held.tile([P, KB, N], F32, name="gate_sb")
 
         nc.sync.dma_start(offsets[:], offs)
-        nc.gpsimd.dma_start(b1_sb[:], b1_v)
-        nc.gpsimd.dma_start(b2_sb[:], b2_v)
-        nc.sync.dma_start(pos_sb[:, 0:HALF, :], pos_v[:, 0:HALF, :])
-        nc.scalar.dma_start(table_sb[0][:], table_v[:, 0, :])
-        nc.sync.dma_start(table_sb[1][:], table_v[:, 1, :])
-        nc.scalar.dma_start(table_sb[2][:], table_v[:, 2, :])
-        nc.sync.dma_start(table_sb[3][:], table_v[:, 3, :])
-        nc.scalar.dma_start(w1_sb[:], w1_v)
-        nc.sync.dma_start(pos_sb[:, HALF:KB, :], pos_v[:, HALF:KB, :])
-        nc.scalar.dma_start(table_sb[4][:], table_v[:, 4, :])
-        nc.sync.dma_start(table_sb[5][:], table_v[:, 5, :])
-        nc.scalar.dma_start(table_sb[6][:], table_v[:, 6, :])
-        nc.sync.dma_start(table_sb[7][:], table_v[:, 7, :])
-        nc.scalar.dma_start(w2_sb[:, 0, :, :], w2_v[:, 0, :, :])
-        nc.sync.dma_start(w2_sb[:, 1, :, :], w2_v[:, 1, :, :])
+        nc.gpsimd.dma_start(w1_sb[:], w1_v)
+        nc.gpsimd.dma_start(w2_sb[:], w2_v)
+        for k in range(KB):
+            if k % HALF == 0:
+                nc.sync.dma_start(pos_sb[:, k : k + HALF, :], pos_v[:, k : k + HALF, :])
+            nc.sync.dma_start(table_sb[k][:], table_v[:, k, :])
+        nc.sync.dma_start(b1_sb[:], b1_v)
+        nc.sync.dma_start(b2_sb[:], b2_v)
+
+        scratch = held.tile([P, 1], F32, name="scratch")
+        nc.vector.memset(scratch[:], 0.0)
+        nc.scalar.activation(scratch[:], scratch[:], SIGMOID)
 
         h_ps = [h_psum.tile([P, N], F32, name=f"h_ps{t}") for t in range(TB)]
         for k in range(KB):

@@ -44,14 +44,16 @@ def tile_quantumtransformer_kernel(tc, table, pos, w1, b1, w2, b2, offs, out):
         gate_sb = held.tile([P, KB, N], F32, name="gate_sb")
 
         nc.sync.dma_start(offsets[:], offs)
-        nc.gpsimd.dma_start(w1_sb[:], w1_v)
-        nc.gpsimd.dma_start(w2_sb[:], w2_v)
-        for k in range(KB):
-            if k % HALF == 0:
-                nc.sync.dma_start(pos_sb[:, k : k + HALF, :], pos_v[:, k : k + HALF, :])
+        nc.sync.dma_start(pos_sb[:, 0:HALF, :], pos_v[:, 0:HALF, :])
+        for k in range(HALF):
             nc.sync.dma_start(table_sb[k][:], table_v[:, k, :])
-        nc.sync.dma_start(b1_sb[:], b1_v)
-        nc.sync.dma_start(b2_sb[:], b2_v)
+        nc.sync.dma_start(w1_sb[:], w1_v)
+        nc.sync.dma_start(pos_sb[:, HALF:KB, :], pos_v[:, HALF:KB, :])
+        for k in range(HALF, KB):
+            nc.sync.dma_start(table_sb[k][:], table_v[:, k, :])
+        nc.sync.dma_start(w2_sb[:], w2_v)
+        nc.gpsimd.dma_start(b1_sb[:], b1_v)
+        nc.gpsimd.dma_start(b2_sb[:], b2_v)
 
         scratch = held.tile([P, 1], F32, name="scratch")
         nc.vector.memset(scratch[:], 0.0)

@@ -30,6 +30,7 @@ def tile_quantumtransformer_kernel(tc, table, pos, w1, b1, w2, b2, offs, out):
         tc.tile_pool(name="held", bufs=1) as held,
         tc.psum_pool(name="h_psum", bufs=1) as h_psum,
         tc.psum_pool(name="g_psum", bufs=4) as g_psum,
+        tc.psum_pool(name="idle_psum", bufs=1) as idle_psum,
     ):
         offsets = held.tile([P, N // 16], U16, name="offsets")
         table_sb = [held.tile([P, S], F32, name=f"table{k}") for k in range(KB)]
@@ -60,6 +61,7 @@ def tile_quantumtransformer_kernel(tc, table, pos, w1, b1, w2, b2, offs, out):
         nc.scalar.activation(scratch[:], scratch[:], SIGMOID)
 
         h_ps = [h_psum.tile([P, N], F32, name=f"h_ps{t}") for t in range(TB)]
+        unread_ps = idle_psum.tile([P, 2, N], F32, name="unread_ps")
         for k in range(KB):
             nc.vector.tensor_tensor(
                 x_sb[:, k, :], table_sb[k][:].indirect(offsets[:]), pos_sb[:, k, :], ADD
@@ -69,6 +71,10 @@ def tile_quantumtransformer_kernel(tc, table, pos, w1, b1, w2, b2, offs, out):
                 nc.tensor.matmul(
                     h_ps[t][:], w1_sb[:, k, :, t], x_bf[:, k, :],
                     start=(k == 0), stop=(k == KB - 1),
+                )
+            if 0 < k < KB - 1:
+                nc.tensor.matmul(
+                    unread_ps[:], x_bf[:, k, :], x_bf[:, k - 1 : k + 1, :], start=True, stop=True
                 )
 
         nc.sync.dma_start(x_out_v, x_sb[:])

@@ -10,6 +10,7 @@ C, R, S, N = 1024, 256, 256, 128
 KB = C // P
 TB = R // P
 HALF = KB // 2
+PAIR = 2
 
 FLOPS = 2 * C * R * N * 2
 
@@ -30,7 +31,6 @@ def tile_quantumtransformer_kernel(tc, table, pos, w1, b1, w2, b2, offs, out):
         tc.tile_pool(name="held", bufs=1) as held,
         tc.psum_pool(name="h_psum", bufs=1) as h_psum,
         tc.psum_pool(name="g_psum", bufs=4) as g_psum,
-        tc.psum_pool(name="idle_psum", bufs=1) as idle_psum,
     ):
         offsets = held.tile([P, N // 16], U16, name="offsets")
         table_sb = [held.tile([P, S], F32, name=f"table{k}") for k in range(KB)]
@@ -61,7 +61,6 @@ def tile_quantumtransformer_kernel(tc, table, pos, w1, b1, w2, b2, offs, out):
         nc.scalar.activation(scratch[:], scratch[:], SIGMOID)
 
         h_ps = [h_psum.tile([P, N], F32, name=f"h_ps{t}") for t in range(TB)]
-        unread_ps = idle_psum.tile([P, 2, N], F32, name="unread_ps")
         for k in range(KB):
             nc.vector.tensor_tensor(
                 x_sb[:, k, :], table_sb[k][:].indirect(offsets[:]), pos_sb[:, k, :], ADD
@@ -71,10 +70,6 @@ def tile_quantumtransformer_kernel(tc, table, pos, w1, b1, w2, b2, offs, out):
                 nc.tensor.matmul(
                     h_ps[t][:], w1_sb[:, k, :, t], x_bf[:, k, :],
                     start=(k == 0), stop=(k == KB - 1),
-                )
-            if 0 < k < KB - 1:
-                nc.tensor.matmul(
-                    unread_ps[:], x_bf[:, k, :], x_bf[:, k - 1 : k + 1, :], start=True, stop=True
                 )
 
         nc.sync.dma_start(x_out_v, x_sb[:])
@@ -90,6 +85,6 @@ def tile_quantumtransformer_kernel(tc, table, pos, w1, b1, w2, b2, offs, out):
                     start=(t == 0), stop=(t == TB - 1),
                 )
             nc.scalar.activation(gate_sb[:, k, :], g_ps[:], SIGMOID, bias=b2_sb[:, k : k + 1])
-            if k % HALF == HALF - 1:
-                blocks = slice(k + 1 - HALF, k + 1)
+            if k % PAIR == PAIR - 1:
+                blocks = slice(k + 1 - PAIR, k + 1)
                 nc.sync.dma_start(gate_out_v[:, blocks, :], gate_sb[:, blocks, :])

@@ -10,7 +10,6 @@ C, R, S, N = 1024, 256, 256, 128
 KB = C // P
 TB = R // P
 HALF = KB // 2
-PAIR = 2
 
 FLOPS = 2 * C * R * N * 2
 
@@ -45,11 +44,10 @@ def tile_quantumtransformer_kernel(tc, table, pos, w1, b1, w2, b2, offs, out):
         gate_sb = held.tile([P, KB, N], F32, name="gate_sb")
 
         nc.sync.dma_start(offsets[:], offs)
-        nc.sync.dma_start(pos_sb[:, 0:HALF, :], pos_v[:, 0:HALF, :])
+        nc.sync.dma_start(pos_sb[:], pos_v)
         for k in range(HALF):
             nc.sync.dma_start(table_sb[k][:], table_v[:, k, :])
         nc.sync.dma_start(w1_sb[:], w1_v)
-        nc.sync.dma_start(pos_sb[:, HALF:KB, :], pos_v[:, HALF:KB, :])
         for k in range(HALF, KB):
             nc.sync.dma_start(table_sb[k][:], table_v[:, k, :])
         nc.sync.dma_start(w2_sb[:], w2_v)
@@ -85,6 +83,6 @@ def tile_quantumtransformer_kernel(tc, table, pos, w1, b1, w2, b2, offs, out):
                     start=(t == 0), stop=(t == TB - 1),
                 )
             nc.scalar.activation(gate_sb[:, k, :], g_ps[:], SIGMOID, bias=b2_sb[:, k : k + 1])
-            if k % PAIR == PAIR - 1:
-                blocks = slice(k + 1 - PAIR, k + 1)
+            if k % HALF == HALF - 1:
+                blocks = slice(k + 1 - HALF, k + 1)
                 nc.sync.dma_start(gate_out_v[:, blocks, :], gate_sb[:, blocks, :])

@@ -10,6 +10,7 @@ C, R, S, N = 1024, 256, 256, 128
 KB = C // P
 TB = R // P
 HALF = KB // 2
+LATE = 2
 
 FLOPS = 2 * C * R * N * 2
 
@@ -47,9 +48,10 @@ def tile_quantumtransformer_kernel(tc, table, pos, w1, b1, w2, b2, offs, out):
         nc.sync.dma_start(pos_sb[:], pos_v)
         for k in range(HALF):
             nc.sync.dma_start(table_sb[k][:], table_v[:, k, :])
-        nc.sync.dma_start(w1_sb[:], w1_v)
+        nc.sync.dma_start(w1_sb[:, 0 : KB - LATE], w1_v[:, 0 : KB - LATE])
         for k in range(HALF, KB):
             nc.sync.dma_start(table_sb[k][:], table_v[:, k, :])
+        nc.sync.dma_start(w1_sb[:, KB - LATE : KB], w1_v[:, KB - LATE : KB])
         nc.sync.dma_start(w2_sb[:], w2_v)
         nc.gpsimd.dma_start(b1_sb[:], b1_v)
         nc.gpsimd.dma_start(b2_sb[:], b2_v)

@@ -10,7 +10,7 @@ C, R, S, N = 1024, 256, 256, 128
 KB = C // P
 TB = R // P
 HALF = KB // 2
-LATE = 2
+LATE = 3
 
 FLOPS = 2 * C * R * N * 2
 

@@ -45,11 +45,12 @@ def tile_quantumtransformer_kernel(tc, table, pos, w1, b1, w2, b2, offs, out):
         gate_sb = held.tile([P, KB, N], F32, name="gate_sb")
 
         nc.sync.dma_start(offsets[:], offs)
-        nc.sync.dma_start(pos_sb[:], pos_v)
-        for k in range(HALF):
-            nc.sync.dma_start(table_sb[k][:], table_v[:, k, :])
-        nc.sync.dma_start(w1_sb[:, 0 : KB - LATE], w1_v[:, 0 : KB - LATE])
-        for k in range(HALF, KB):
+        nc.sync.dma_start(table_sb[0][:], table_v[:, 0, :])
+        nc.sync.dma_start(table_sb[1][:], table_v[:, 1, :])
+        nc.scalar.dma_start(pos_sb[:], pos_v)
+        nc.sync.dma_start(table_sb[2][:], table_v[:, 2, :])
+        nc.scalar.dma_start(w1_sb[:, 0 : KB - LATE], w1_v[:, 0 : KB - LATE])
+        for k in range(3, KB):
             nc.sync.dma_start(table_sb[k][:], table_v[:, k, :])
         nc.sync.dma_start(w1_sb[:, KB - LATE : KB], w1_v[:, KB - LATE : KB])
         nc.sync.dma_start(w2_sb[:], w2_v)

@@ -11,6 +11,7 @@ KB = C // P
 TB = R // P
 HALF = KB // 2
 LATE = 3
+PAIR = 2
 
 FLOPS = 2 * C * R * N * 2
 
@@ -78,14 +79,21 @@ def tile_quantumtransformer_kernel(tc, table, pos, w1, b1, w2, b2, offs, out):
         for t in range(TB):
             nc.scalar.activation(h_bf[:, t, :], h_ps[t][:], TANH, bias=b1_sb[:, t : t + 1])
 
-        for k in range(KB):
-            g_ps = g_psum.tile([P, N], F32, name="g_ps")
+        for first in range(0, KB, PAIR):
+            g_ps = [g_psum.tile([P, N], F32, name="g_ps") for k in range(PAIR)]
             for t in range(TB):
-                nc.tensor.matmul(
-                    g_ps[:], w2_sb[:, t, :, k], h_bf[:, t, :],
-                    start=(t == 0), stop=(t == TB - 1),
+                for k in range(PAIR):
+                    nc.tensor.matmul(
+                        g_ps[k][:], w2_sb[:, t, :, first + k], h_bf[:, t, :],
+                        start=(t == 0), stop=(t == TB - 1),
+                    )
+            for k in range(PAIR):
+                nc.scalar.activation(
+                    gate_sb[:, first + k, :], g_ps[k][:], SIGMOID,
+                    bias=b2_sb[:, first + k : first + k + 1],
                 )
-            nc.scalar.activation(gate_sb[:, k, :], g_ps[:], SIGMOID, bias=b2_sb[:, k : k + 1])
-            if k % HALF == HALF - 1:
-                blocks = slice(k + 1 - HALF, k + 1)
-                nc.sync.dma_start(gate_out_v[:, blocks, :], gate_sb[:, blocks, :])
+            done = first + PAIR
+            if done % HALF == 0:
+                nc.sync.dma_start(
+                    gate_out_v[:, done - HALF : done, :], gate_sb[:, done - HALF : done, :]
+                )

import concourse.mybir as mybir

F32, BF16, U16 = mybir.dt.float32, mybir.dt.bfloat16, mybir.dt.uint16
ADD = mybir.AluOpType.add
TANH = mybir.ActivationFunctionType.Tanh
SIGMOID = mybir.ActivationFunctionType.Sigmoid

P = 128
C, R, S, N = 1024, 256, 256, 128
KB = C // P
TB = R // P
HALF = KB // 2
LATE = 3
PAIR = 2

FLOPS = 2 * C * R * N * 2


def tile_quantumtransformer_kernel(tc, table, pos, w1, b1, w2, b2, offs, out):
    nc = tc.nc

    table_v = table.rearrange("(p k) s -> p k s", k=KB)
    pos_v = pos.rearrange("(p k) j -> p k j", k=KB)
    w1_v = w1.rearrange("(p k) (m t) -> p k m t", k=KB, t=TB)
    w2_v = w2.rearrange("(p t) (m k) -> p t m k", t=TB, k=KB)
    b1_v = b1.rearrange("(p t) one -> p (t one)", t=TB)
    b2_v = b2.rearrange("(p k) one -> p (k one)", k=KB)
    x_out_v = out[0:C, :].rearrange("(p k) j -> p k j", k=KB)
    gate_out_v = out[C : 2 * C, :].rearrange("(p k) j -> p k j", k=KB)

    with (
        tc.tile_pool(name="held", bufs=1) as held,
        tc.psum_pool(name="h_psum", bufs=1) as h_psum,
        tc.psum_pool(name="g_psum", bufs=4) as g_psum,
    ):
        offsets = held.tile([P, N // 16], U16, name="offsets")
        table_sb = [held.tile([P, S], F32, name=f"table{k}") for k in range(KB)]
        pos_sb = held.tile([P, KB, N], F32, name="pos_sb")
        w1_sb = held.tile([P, KB, P, TB], BF16, name="w1_sb")
        w2_sb = held.tile([P, TB, P, KB], BF16, name="w2_sb")
        b1_sb = held.tile([P, TB], F32, name="b1_sb")
        b2_sb = held.tile([P, KB], F32, name="b2_sb")
        x_sb = held.tile([P, KB, N], F32, name="x_sb")
        x_bf = held.tile([P, KB, N], BF16, name="x_bf")
        h_bf = held.tile([P, TB, N], BF16, name="h_bf")
        gate_sb = held.tile([P, KB, N], F32, name="gate_sb")

        nc.sync.dma_start(offsets[:], offs)
        nc.sync.dma_start(table_sb[0][:], table_v[:, 0, :])
        nc.sync.dma_start(table_sb[1][:], table_v[:, 1, :])
        nc.scalar.dma_start(pos_sb[:], pos_v)
        nc.sync.dma_start(table_sb[2][:], table_v[:, 2, :])
        nc.scalar.dma_start(w1_sb[:, 0 : KB - LATE], w1_v[:, 0 : KB - LATE])
        for k in range(3, KB):
            nc.sync.dma_start(table_sb[k][:], table_v[:, k, :])
        nc.sync.dma_start(w1_sb[:, KB - LATE : KB], w1_v[:, KB - LATE : KB])
        nc.sync.dma_start(w2_sb[:], w2_v)
        nc.gpsimd.dma_start(b1_sb[:], b1_v)
        nc.gpsimd.dma_start(b2_sb[:], b2_v)

        scratch = held.tile([P, 1], F32, name="scratch")
        nc.vector.memset(scratch[:], 0.0)
        nc.scalar.activation(scratch[:], scratch[:], SIGMOID)

        h_ps = [h_psum.tile([P, N], F32, name=f"h_ps{t}") for t in range(TB)]
        for k in range(KB):
            nc.vector.tensor_tensor(
                x_sb[:, k, :], table_sb[k][:].indirect(offsets[:]), pos_sb[:, k, :], ADD
            )
            nc.scalar.copy(x_bf[:, k, :], x_sb[:, k, :])
            for t in range(TB):
                nc.tensor.matmul(
                    h_ps[t][:], w1_sb[:, k, :, t], x_bf[:, k, :],
                    start=(k == 0), stop=(k == KB - 1),
                )

        nc.sync.dma_start(x_out_v, x_sb[:])

        for t in range(TB):
            nc.scalar.activation(h_bf[:, t, :], h_ps[t][:], TANH, bias=b1_sb[:, t : t + 1])

        for first in range(0, KB, PAIR):
            g_ps = [g_psum.tile([P, N], F32, name="g_ps") for k in range(PAIR)]
            for t in range(TB):
                for k in range(PAIR):
                    nc.tensor.matmul(
                        g_ps[k][:], w2_sb[:, t, :, first + k], h_bf[:, t, :],
                        start=(t == 0), stop=(t == TB - 1),
                    )
            for k in range(PAIR):
                nc.scalar.activation(
                    gate_sb[:, first + k, :], g_ps[k][:], SIGMOID,
                    bias=b2_sb[:, first + k : first + k + 1],
                )
            done = first + PAIR
            if done % HALF == 0:
                nc.sync.dma_start(
                    gate_out_v[:, done - HALF : done, :], gate_sb[:, done - HALF : done, :]
                )
